import numpy as np
import ml_dtypes

BF16 = ml_dtypes.bfloat16


def bf(x):
    return np.asarray(x, np.float32).astype(BF16)


def f32(x):
    return np.asarray(x, np.float32)


def f64(x):
    return np.asarray(x).astype(np.float64)


def striped(idx):
    return np.tile(idx.reshape(-1, 16).T, (8, 1))


C, S, N, NG, NN, K = 512, 1024, 4096, 4, 32, 8


def setup_inputs():
    idx = np.concatenate([np.random.permutation(S)[:S // 2] for _ in range(K)])
    return {
        "feat": bf(np.random.standard_normal((C, NG * NN))),
        "w0": bf(np.random.standard_normal((C, C)) / np.sqrt(C)),
        "b0": f32(0.1 * np.random.standard_normal((C, 1))),
        "w1": bf(np.random.standard_normal((C, C)) / np.sqrt(C)),
        "b1": f32(0.1 * np.random.standard_normal((C, 1))),
        "emb_tf": f32(np.random.standard_normal((C, S))),
        "offs": striped(idx),
    }


def reference(feat, w0, b0, w1, b1, emb_tf, offs):
    idx = offs[:16].T.reshape(-1)
    x0 = (f64(w0).T @ f64(feat) + f64(b0)).reshape(C, NG, NN)
    x1 = (f64(w1).T @ f64(feat) + f64(b1)).reshape(C, NG, NN)
    pair = (x0[:, :, :, None] * x1[:, :, None, :]).reshape(C, N)
    return f64(emb_tf)[:, idx] * pair

@@ -1,0 +1,75 @@
+import concourse.mybir as mybir
+
+BF16, F32, U16 = mybir.dt.bfloat16, mybir.dt.float32, mybir.dt.uint16
+MULT = mybir.AluOpType.mult
+
+P = 128
+CHANNELS = 512
+CODES = 1024
+GRAPHS = 4
+NODES = 32
+ALL_NODES = GRAPHS * NODES
+PAIRS = NODES * NODES
+LIST = GRAPHS * PAIRS
+BLOCKS = CHANNELS // P
+
+FLOPS = 2 * 2 * CHANNELS * CHANNELS * ALL_NODES
+
+
+def tile_spmodel_kernel(tc, feat, w0, b0, w1, b1, emb_tf, offs, out):
+    nc = tc.nc
+    with (
+        tc.tile_pool(name="held", bufs=1) as held,
+        tc.tile_pool(name="proj", bufs=2) as proj,
+        tc.tile_pool(name="ring", bufs=4) as ring,
+        tc.psum_pool(name="psum", bufs=2) as psum,
+    ):
+        offsets = held.tile([P, LIST // 16], U16, name="offsets")
+        nc.sync.dma_start(offsets[:], offs)
+
+        feat_sb = held.tile([P, BLOCKS, ALL_NODES], BF16, name="feat_sb")
+        nc.sync.dma_start(feat_sb[:], feat.rearrange("(k p) n -> p k n", p=P))
+        w_sb = [held.tile([P, BLOCKS, CHANNELS], BF16, name=f"w{i}_sb") for i in range(2)]
+        nc.scalar.dma_start(w_sb[0][:], w0.rearrange("(k p) c -> p k c", p=P))
+        nc.gpsimd.dma_start(w_sb[1][:], w1.rearrange("(k p) c -> p k c", p=P))
+
+        b_row = [held.tile([1, CHANNELS], F32, name=f"b{i}_row") for i in range(2)]
+        nc.scalar.dma_start(b_row[0][:], b0.rearrange("c o -> o c"))
+        nc.gpsimd.dma_start(b_row[1][:], b1.rearrange("c o -> o c"))
+        ones = held.tile([1, ALL_NODES], F32, name="ones")
+        nc.vector.memset(ones[:], 1.0)
+
+        emb = [held.tile([P, CODES], F32, name=f"emb{cb}") for cb in range(BLOCKS)]
+        for cb in range(BLOCKS):
+            nc.sync.dma_start(emb[cb][:], emb_tf[cb * P : (cb + 1) * P, :])
+
+        for cb in range(BLOCKS):
+            channels = slice(cb * P, (cb + 1) * P)
+
+            x = []
+            for i in range(2):
+                acc = psum.tile([P, ALL_NODES], F32, name=f"acc{i}")
+                nc.tensor.matmul(acc[:], b_row[i][:, channels], ones[:], start=True, stop=False)
+                for k in range(BLOCKS):
+                    nc.tensor.matmul(
+                        acc[:], w_sb[i][:, k, channels], feat_sb[:, k, :], start=False, stop=(k == BLOCKS - 1)
+                    )
+                x_sb = proj.tile([P, ALL_NODES], F32, name=f"x{i}_sb")
+                nc.scalar.copy(x_sb[:], acc[:])
+                x.append(x_sb)
+
+            for r in range(GRAPHS):
+                nodes = slice(r * NODES, (r + 1) * NODES)
+                pair = ring.tile([P, NODES, NODES], F32, name="pair")
+                nc.gpsimd.tensor_tensor(
+                    pair[:],
+                    x[0][:, nodes].unsqueeze(2).to_broadcast([P, NODES, NODES]),
+                    x[1][:, nodes].unsqueeze(1).to_broadcast([P, NODES, NODES]),
+                    MULT,
+                )
+                piece = offsets[:, r * (PAIRS // 16) : (r + 1) * (PAIRS // 16)]
+                prod = ring.tile([P, PAIRS], F32, name="prod")
+                nc.vector.tensor_tensor(
+                    prod[:], emb[cb][:].indirect(piece), pair[:].rearrange("p a t -> p (a t)"), MULT
+                )
+                nc.sync.dma_start(out[channels, r * PAIRS : (r + 1) * PAIRS], prod[:])

@@ -2,6 +2,7 @@ import concourse.mybir as mybir
 
 BF16, F32, U16 = mybir.dt.bfloat16, mybir.dt.float32, mybir.dt.uint16
 MULT = mybir.AluOpType.mult
+COPY = mybir.ActivationFunctionType.Copy
 
 P = 128
 CHANNELS = 512
@@ -60,16 +61,15 @@ def tile_spmodel_kernel(tc, feat, w0, b0, w1, b1, emb_tf, offs, out):
 
             for r in range(GRAPHS):
                 nodes = slice(r * NODES, (r + 1) * NODES)
-                pair = ring.tile([P, NODES, NODES], F32, name="pair")
-                nc.gpsimd.tensor_tensor(
-                    pair[:],
-                    x[0][:, nodes].unsqueeze(2).to_broadcast([P, NODES, NODES]),
-                    x[1][:, nodes].unsqueeze(1).to_broadcast([P, NODES, NODES]),
-                    MULT,
-                )
+                pair = ring.tile([P, PAIRS], F32, name="pair")
+                for a in range(NODES):
+                    first = r * NODES + a
+                    nc.scalar.activation(
+                        pair[:, a * NODES : (a + 1) * NODES], x[1][:, nodes], COPY, scale=x[0][:, first : first + 1]
+                    )
                 piece = offsets[:, r * (PAIRS // 16) : (r + 1) * (PAIRS // 16)]
                 prod = ring.tile([P, PAIRS], F32, name="prod")
                 nc.vector.tensor_tensor(
-                    prod[:], emb[cb][:].indirect(piece), pair[:].rearrange("p a t -> p (a t)"), MULT
+                    prod[:], emb[cb][:].indirect(piece), pair[:], MULT
                 )
                 nc.sync.dma_start(out[channels, r * PAIRS : (r + 1) * PAIRS], prod[:])

@@ -25,24 +25,26 @@ def tile_spmodel_kernel(tc, feat, w0, b0, w1, b1, emb_tf, offs, out):
         tc.tile_pool(name="ring", bufs=4) as ring,
         tc.psum_pool(name="psum", bufs=2) as psum,
     ):
-        offsets = held.tile([P, LIST // 16], U16, name="offsets")
-        nc.sync.dma_start(offsets[:], offs)
-
         feat_sb = held.tile([P, BLOCKS, ALL_NODES], BF16, name="feat_sb")
         nc.sync.dma_start(feat_sb[:], feat.rearrange("(k p) n -> p k n", p=P))
-        w_sb = [held.tile([P, BLOCKS, CHANNELS], BF16, name=f"w{i}_sb") for i in range(2)]
-        nc.scalar.dma_start(w_sb[0][:], w0.rearrange("(k p) c -> p k c", p=P))
-        nc.gpsimd.dma_start(w_sb[1][:], w1.rearrange("(k p) c -> p k c", p=P))
 
         b_row = [held.tile([1, CHANNELS], F32, name=f"b{i}_row") for i in range(2)]
-        nc.scalar.dma_start(b_row[0][:], b0.rearrange("c o -> o c"))
-        nc.gpsimd.dma_start(b_row[1][:], b1.rearrange("c o -> o c"))
+        for i, b in enumerate((b0, b1)):
+            nc.sync.dma_start(b_row[i][:], b.rearrange("c o -> o c"))
         ones = held.tile([1, ALL_NODES], F32, name="ones")
         nc.vector.memset(ones[:], 1.0)
 
+        offsets = held.tile([P, LIST // 16], U16, name="offsets")
+
+        w_sb = [[held.tile([P, BLOCKS, P], BF16, name=f"w{i}_sb{cb}") for cb in range(BLOCKS)] for i in range(2)]
         emb = [held.tile([P, CODES], F32, name=f"emb{cb}") for cb in range(BLOCKS)]
         for cb in range(BLOCKS):
-            nc.sync.dma_start(emb[cb][:], emb_tf[cb * P : (cb + 1) * P, :])
+            channels = slice(cb * P, (cb + 1) * P)
+            for i, w in enumerate((w0, w1)):
+                nc.sync.dma_start(w_sb[i][cb][:], w[:, channels].rearrange("(k p) c -> p k c", p=P))
+            if cb == 0:
+                nc.sync.dma_start(offsets[:], offs)
+            nc.sync.dma_start(emb[cb][:], emb_tf[channels, :])
 
         for cb in range(BLOCKS):
             channels = slice(cb * P, (cb + 1) * P)
@@ -53,7 +55,7 @@ def tile_spmodel_kernel(tc, feat, w0, b0, w1, b1, emb_tf, offs, out):
                 nc.tensor.matmul(acc[:], b_row[i][:, channels], ones[:], start=True, stop=False)
                 for k in range(BLOCKS):
                     nc.tensor.matmul(
-                        acc[:], w_sb[i][:, k, channels], feat_sb[:, k, :], start=False, stop=(k == BLOCKS - 1)
+                        acc[:], w_sb[i][cb][:, k, :], feat_sb[:, k, :], start=False, stop=(k == BLOCKS - 1)
                     )
                 x_sb = proj.tile([P, ALL_NODES], F32, name=f"x{i}_sb")
                 nc.scalar.copy(x_sb[:], acc[:])
@@ -69,7 +71,5 @@ def tile_spmodel_kernel(tc, feat, w0, b0, w1, b1, emb_tf, offs, out):
                     )
                 piece = offsets[:, r * (PAIRS // 16) : (r + 1) * (PAIRS // 16)]
                 prod = ring.tile([P, PAIRS], F32, name="prod")
-                nc.vector.tensor_tensor(
-                    prod[:], emb[cb][:].indirect(piece), pair[:], MULT
-                )
+                nc.vector.tensor_tensor(prod[:], emb[cb][:].indirect(piece), pair[:], MULT)
                 nc.sync.dma_start(out[channels, r * PAIRS : (r + 1) * PAIRS], prod[:])

@@ -26,11 +26,9 @@ def tile_spmodel_kernel(tc, feat, w0, b0, w1, b1, emb_tf, offs, out):
         tc.psum_pool(name="psum", bufs=2) as psum,
     ):
         feat_sb = held.tile([P, BLOCKS, ALL_NODES], BF16, name="feat_sb")
-        nc.sync.dma_start(feat_sb[:], feat.rearrange("(k p) n -> p k n", p=P))
+        nc.sync.dma_start(feat_sb[:], feat.rearrange("(p k) n -> p k n", p=P))
 
         b_row = [held.tile([1, CHANNELS], F32, name=f"b{i}_row") for i in range(2)]
-        for i, b in enumerate((b0, b1)):
-            nc.sync.dma_start(b_row[i][:], b.rearrange("c o -> o c"))
         ones = held.tile([1, ALL_NODES], F32, name="ones")
         nc.vector.memset(ones[:], 1.0)
 
@@ -40,10 +38,12 @@ def tile_spmodel_kernel(tc, feat, w0, b0, w1, b1, emb_tf, offs, out):
         emb = [held.tile([P, CODES], F32, name=f"emb{cb}") for cb in range(BLOCKS)]
         for cb in range(BLOCKS):
             channels = slice(cb * P, (cb + 1) * P)
-            for i, w in enumerate((w0, w1)):
-                nc.sync.dma_start(w_sb[i][cb][:], w[:, channels].rearrange("(k p) c -> p k c", p=P))
+            nc.sync.dma_start(w_sb[0][cb][:], w0[:, channels].rearrange("(p k) c -> p k c", p=P))
+            nc.sync.dma_start(w_sb[1][cb][:], w1[:, channels].rearrange("(p k) c -> p k c", p=P))
             if cb == 0:
                 nc.sync.dma_start(offsets[:], offs)
+                for i, b in enumerate((b0, b1)):
+                    nc.scalar.dma_start(b_row[i][:], b.rearrange("c o -> o c"))
             nc.sync.dma_start(emb[cb][:], emb_tf[channels, :])
 
         for cb in range(BLOCKS):
@@ -52,11 +52,9 @@ def tile_spmodel_kernel(tc, feat, w0, b0, w1, b1, emb_tf, offs, out):
             x = []
             for i in range(2):
                 acc = psum.tile([P, ALL_NODES], F32, name=f"acc{i}")
-                nc.tensor.matmul(acc[:], b_row[i][:, channels], ones[:], start=True, stop=False)
                 for k in range(BLOCKS):
-                    nc.tensor.matmul(
-                        acc[:], w_sb[i][cb][:, k, :], feat_sb[:, k, :], start=False, stop=(k == BLOCKS - 1)
-                    )
+                    nc.tensor.matmul(acc[:], w_sb[i][cb][:, k, :], feat_sb[:, k, :], start=(k == 0), stop=False)
+                nc.tensor.matmul(acc[:], b_row[i][:, channels], ones[:], start=False, stop=True)
                 x_sb = proj.tile([P, ALL_NODES], F32, name=f"x{i}_sb")
                 nc.scalar.copy(x_sb[:], acc[:])
                 x.append(x_sb)
@@ -64,11 +62,19 @@ def tile_spmodel_kernel(tc, feat, w0, b0, w1, b1, emb_tf, offs, out):
             for r in range(GRAPHS):
                 nodes = slice(r * NODES, (r + 1) * NODES)
                 pair = ring.tile([P, PAIRS], F32, name="pair")
-                for a in range(NODES):
-                    first = r * NODES + a
-                    nc.scalar.activation(
-                        pair[:, a * NODES : (a + 1) * NODES], x[1][:, nodes], COPY, scale=x[0][:, first : first + 1]
+                if cb == 0 and r == 0:
+                    nc.vector.tensor_tensor(
+                        pair[:].rearrange("p (a t) -> p a t", a=NODES),
+                        x[0][:, nodes].unsqueeze(2).to_broadcast([P, NODES, NODES]),
+                        x[1][:, nodes].unsqueeze(1).to_broadcast([P, NODES, NODES]),
+                        MULT,
                     )
+                else:
+                    for a in range(NODES):
+                        first = r * NODES + a
+                        nc.scalar.activation(
+                            pair[:, a * NODES : (a + 1) * NODES], x[1][:, nodes], COPY, scale=x[0][:, first : first + 1]
+                        )
                 piece = offsets[:, r * (PAIRS // 16) : (r + 1) * (PAIRS // 16)]
                 prod = ring.tile([P, PAIRS], F32, name="prod")
                 nc.vector.tensor_tensor(prod[:], emb[cb][:].indirect(piece), pair[:], MULT)

@@ -3,6 +3,7 @@ import concourse.mybir as mybir
 BF16, F32, U16 = mybir.dt.bfloat16, mybir.dt.float32, mybir.dt.uint16
 MULT = mybir.AluOpType.mult
 COPY = mybir.ActivationFunctionType.Copy
+IDENTITY = mybir.ActivationFunctionType.Identity
 
 P = 128
 CHANNELS = 512
@@ -28,9 +29,7 @@ def tile_spmodel_kernel(tc, feat, w0, b0, w1, b1, emb_tf, offs, out):
         feat_sb = held.tile([P, BLOCKS, ALL_NODES], BF16, name="feat_sb")
         nc.sync.dma_start(feat_sb[:], feat.rearrange("(p k) n -> p k n", p=P))
 
-        b_row = [held.tile([1, CHANNELS], F32, name=f"b{i}_row") for i in range(2)]
-        ones = held.tile([1, ALL_NODES], F32, name="ones")
-        nc.vector.memset(ones[:], 1.0)
+        b_sb = [held.tile([P, BLOCKS], F32, name=f"b{i}_sb") for i in range(2)]
 
         offsets = held.tile([P, LIST // 16], U16, name="offsets")
 
@@ -43,7 +42,7 @@ def tile_spmodel_kernel(tc, feat, w0, b0, w1, b1, emb_tf, offs, out):
             if cb == 0:
                 nc.sync.dma_start(offsets[:], offs)
                 for i, b in enumerate((b0, b1)):
-                    nc.scalar.dma_start(b_row[i][:], b.rearrange("c o -> o c"))
+                    nc.scalar.dma_start(b_sb[i][:], b.rearrange("(a p) o -> p (a o)", p=P))
             nc.sync.dma_start(emb[cb][:], emb_tf[channels, :])
 
         for cb in range(BLOCKS):
@@ -53,10 +52,9 @@ def tile_spmodel_kernel(tc, feat, w0, b0, w1, b1, emb_tf, offs, out):
             for i in range(2):
                 acc = psum.tile([P, ALL_NODES], F32, name=f"acc{i}")
                 for k in range(BLOCKS):
-                    nc.tensor.matmul(acc[:], w_sb[i][cb][:, k, :], feat_sb[:, k, :], start=(k == 0), stop=False)
-                nc.tensor.matmul(acc[:], b_row[i][:, channels], ones[:], start=False, stop=True)
+                    nc.tensor.matmul(acc[:], w_sb[i][cb][:, k, :], feat_sb[:, k, :], start=(k == 0), stop=(k == BLOCKS - 1))
                 x_sb = proj.tile([P, ALL_NODES], F32, name=f"x{i}_sb")
-                nc.scalar.copy(x_sb[:], acc[:])
+                nc.scalar.activation(x_sb[:], acc[:], IDENTITY, bias=b_sb[i][:, cb : cb + 1])
                 x.append(x_sb)
 
             for r in range(GRAPHS):

@@ -2,7 +2,6 @@ import concourse.mybir as mybir
 
 BF16, F32, U16 = mybir.dt.bfloat16, mybir.dt.float32, mybir.dt.uint16
 MULT = mybir.AluOpType.mult
-COPY = mybir.ActivationFunctionType.Copy
 IDENTITY = mybir.ActivationFunctionType.Identity
 
 P = 128
@@ -14,8 +13,10 @@ ALL_NODES = GRAPHS * NODES
 PAIRS = NODES * NODES
 LIST = GRAPHS * PAIRS
 BLOCKS = CHANNELS // P
+STRIPE = 16
 
 FLOPS = 2 * 2 * CHANNELS * CHANNELS * ALL_NODES
+LAST = NODES // 4
 
 
 def tile_spmodel_kernel(tc, feat, w0, b0, w1, b1, emb_tf, offs, out):
@@ -26,12 +27,17 @@ def tile_spmodel_kernel(tc, feat, w0, b0, w1, b1, emb_tf, offs, out):
         tc.tile_pool(name="ring", bufs=4) as ring,
         tc.psum_pool(name="psum", bufs=2) as psum,
     ):
+        zero = held.tile([P, 1], F32, name="zero")
+        warm = held.tile([P, 1], F32, name="warm")
+        nc.vector.memset(zero[:], 0.0)
+        nc.scalar.activation(warm[:], zero[:], IDENTITY)
+
         feat_sb = held.tile([P, BLOCKS, ALL_NODES], BF16, name="feat_sb")
         nc.sync.dma_start(feat_sb[:], feat.rearrange("(p k) n -> p k n", p=P))
 
         b_sb = [held.tile([P, BLOCKS], F32, name=f"b{i}_sb") for i in range(2)]
 
-        offsets = held.tile([P, LIST // 16], U16, name="offsets")
+        offsets = held.tile([P, LIST // STRIPE], U16, name="offsets")
 
         w_sb = [[held.tile([P, BLOCKS, P], BF16, name=f"w{i}_sb{cb}") for cb in range(BLOCKS)] for i in range(2)]
         emb = [held.tile([P, CODES], F32, name=f"emb{cb}") for cb in range(BLOCKS)]
@@ -45,9 +51,7 @@ def tile_spmodel_kernel(tc, feat, w0, b0, w1, b1, emb_tf, offs, out):
                     nc.scalar.dma_start(b_sb[i][:], b.rearrange("(a p) o -> p (a o)", p=P))
             nc.sync.dma_start(emb[cb][:], emb_tf[channels, :])
 
-        for cb in range(BLOCKS):
-            channels = slice(cb * P, (cb + 1) * P)
-
+        def project(cb):
             x = []
             for i in range(2):
                 acc = psum.tile([P, ALL_NODES], F32, name=f"acc{i}")
@@ -56,24 +60,38 @@ def tile_spmodel_kernel(tc, feat, w0, b0, w1, b1, emb_tf, offs, out):
                 x_sb = proj.tile([P, ALL_NODES], F32, name=f"x{i}_sb")
                 nc.scalar.activation(x_sb[:], acc[:], IDENTITY, bias=b_sb[i][:, cb : cb + 1])
                 x.append(x_sb)
+            return x
 
-            for r in range(GRAPHS):
-                nodes = slice(r * NODES, (r + 1) * NODES)
-                pair = ring.tile([P, PAIRS], F32, name="pair")
-                if cb == 0 and r == 0:
-                    nc.vector.tensor_tensor(
-                        pair[:].rearrange("p (a t) -> p a t", a=NODES),
-                        x[0][:, nodes].unsqueeze(2).to_broadcast([P, NODES, NODES]),
-                        x[1][:, nodes].unsqueeze(1).to_broadcast([P, NODES, NODES]),
-                        MULT,
+        def piece(cb, x, r, a0, many, pair_on_vector=False):
+            nodes = slice(r * NODES, (r + 1) * NODES)
+            width = many * NODES
+            start = r * PAIRS + a0 * NODES
+            pair = ring.tile([P, width], F32, name="pair")
+            if pair_on_vector:
+                nc.vector.tensor_tensor(
+                    pair[:].rearrange("p (a t) -> p a t", a=many),
+                    x[0][:, r * NODES + a0 : r * NODES + a0 + many].unsqueeze(2).to_broadcast([P, many, NODES]),
+                    x[1][:, nodes].unsqueeze(1).to_broadcast([P, many, NODES]),
+                    MULT,
+                )
+            else:
+                for a in range(many):
+                    first = r * NODES + a0 + a
+                    nc.scalar.activation(
+                        pair[:, a * NODES : (a + 1) * NODES], x[1][:, nodes], IDENTITY, scale=x[0][:, first : first + 1]
                     )
+            entries = offsets[:, start // STRIPE : (start + width) // STRIPE]
+            prod = ring.tile([P, width], F32, name="prod")
+            nc.vector.tensor_tensor(prod[:], emb[cb][:].indirect(entries), pair[:], MULT)
+            nc.sync.dma_start(out[cb * P : (cb + 1) * P, start : start + width], prod[:])
+
+        for cb in range(BLOCKS):
+            x = project(cb)
+            for r in range(GRAPHS):
+                if cb == 0 and r == 0:
+                    piece(cb, x, r, 0, NODES, pair_on_vector=True)
+                elif cb == BLOCKS - 1 and r == GRAPHS - 1:
+                    piece(cb, x, r, 0, NODES - LAST)
+                    piece(cb, x, r, NODES - LAST, LAST)
                 else:
-                    for a in range(NODES):
-                        first = r * NODES + a
-                        nc.scalar.activation(
-                            pair[:, a * NODES : (a + 1) * NODES], x[1][:, nodes], COPY, scale=x[0][:, first : first + 1]
-                        )
-                piece = offsets[:, r * (PAIRS // 16) : (r + 1) * (PAIRS // 16)]
-                prod = ring.tile([P, PAIRS], F32, name="prod")
-                nc.vector.tensor_tensor(prod[:], emb[cb][:].indirect(piece), pair[:], MULT)
-                nc.sync.dma_start(out[channels, r * PAIRS : (r + 1) * PAIRS], prod[:])
+                    piece(cb, x, r, 0, NODES)

@@ -89,7 +89,8 @@ def tile_spmodel_kernel(tc, feat, w0, b0, w1, b1, emb_tf, offs, out):
             x = project(cb)
             for r in range(GRAPHS):
                 if cb == 0 and r == 0:
-                    piece(cb, x, r, 0, NODES, pair_on_vector=True)
+                    piece(cb, x, r, 0, NODES // 2, pair_on_vector=True)
+                    piece(cb, x, r, NODES // 2, NODES // 2)
                 elif cb == BLOCKS - 1 and r == GRAPHS - 1:
                     piece(cb, x, r, 0, NODES - LAST)
                     piece(cb, x, r, NODES - LAST, LAST)

@@ -1,7 +1,7 @@
 import concourse.mybir as mybir
 
 BF16, F32, U16 = mybir.dt.bfloat16, mybir.dt.float32, mybir.dt.uint16
-MULT = mybir.AluOpType.mult
+MULT, ADD = mybir.AluOpType.mult, mybir.AluOpType.add
 IDENTITY = mybir.ActivationFunctionType.Identity
 
 P = 128
@@ -27,15 +27,12 @@ def tile_spmodel_kernel(tc, feat, w0, b0, w1, b1, emb_tf, offs, out):
         tc.tile_pool(name="ring", bufs=4) as ring,
         tc.psum_pool(name="psum", bufs=2) as psum,
     ):
-        zero = held.tile([P, 1], F32, name="zero")
-        warm = held.tile([P, 1], F32, name="warm")
-        nc.vector.memset(zero[:], 0.0)
-        nc.scalar.activation(warm[:], zero[:], IDENTITY)
-
         feat_sb = held.tile([P, BLOCKS, ALL_NODES], BF16, name="feat_sb")
         nc.sync.dma_start(feat_sb[:], feat.rearrange("(p k) n -> p k n", p=P))
 
-        b_sb = [held.tile([P, BLOCKS], F32, name=f"b{i}_sb") for i in range(2)]
+        b_sb = [[held.tile([P, 1], F32, name=f"b{i}_sb{cb}") for cb in range(BLOCKS)] for i in range(2)]
+        for i, b in enumerate((b0, b1)):
+            nc.scalar.dma_start(b_sb[i][0][:], b[0:P, :])
 
         offsets = held.tile([P, LIST // STRIPE], U16, name="offsets")
 
@@ -47,9 +44,17 @@ def tile_spmodel_kernel(tc, feat, w0, b0, w1, b1, emb_tf, offs, out):
             nc.sync.dma_start(w_sb[1][cb][:], w1[:, channels].rearrange("(p k) c -> p k c", p=P))
             if cb == 0:
                 nc.sync.dma_start(offsets[:], offs)
-                for i, b in enumerate((b0, b1)):
-                    nc.scalar.dma_start(b_sb[i][:], b.rearrange("(a p) o -> p (a o)", p=P))
             nc.sync.dma_start(emb[cb][:], emb_tf[channels, :])
+        for cb in range(1, BLOCKS):
+            for i, b in enumerate((b0, b1)):
+                nc.sync.dma_start(b_sb[i][cb][:], b[cb * P : (cb + 1) * P, :])
+
+        zero = held.tile([P, 1], F32, name="zero")
+        warm = held.tile([P, 1], F32, name="warm")
+        nc.vector.memset(zero[:], 0.0)
+        nc.scalar.activation(warm[:], zero[:], IDENTITY)
+
+        x_early = [held.tile([P, NODES], F32, name=f"x{i}_early") for i in range(2)]
 
         def project(cb):
             x = []
@@ -57,8 +62,10 @@ def tile_spmodel_kernel(tc, feat, w0, b0, w1, b1, emb_tf, offs, out):
                 acc = psum.tile([P, ALL_NODES], F32, name=f"acc{i}")
                 for k in range(BLOCKS):
                     nc.tensor.matmul(acc[:], w_sb[i][cb][:, k, :], feat_sb[:, k, :], start=(k == 0), stop=(k == BLOCKS - 1))
+                if cb == 0:
+                    nc.vector.tensor_scalar(x_early[i][:], acc[:, 0:NODES], b_sb[i][0][:], None, ADD)
                 x_sb = proj.tile([P, ALL_NODES], F32, name=f"x{i}_sb")
-                nc.scalar.activation(x_sb[:], acc[:], IDENTITY, bias=b_sb[i][:, cb : cb + 1])
+                nc.scalar.activation(x_sb[:], acc[:], IDENTITY, bias=b_sb[i][cb][:])
                 x.append(x_sb)
             return x
 
@@ -89,7 +96,7 @@ def tile_spmodel_kernel(tc, feat, w0, b0, w1, b1, emb_tf, offs, out):
             x = project(cb)
             for r in range(GRAPHS):
                 if cb == 0 and r == 0:
-                    piece(cb, x, r, 0, NODES // 2, pair_on_vector=True)
+                    piece(cb, x_early, r, 0, NODES // 2, pair_on_vector=True)
                     piece(cb, x, r, NODES // 2, NODES // 2)
                 elif cb == BLOCKS - 1 and r == GRAPHS - 1:
                     piece(cb, x, r, 0, NODES - LAST)

@@ -24,7 +24,7 @@ def tile_spmodel_kernel(tc, feat, w0, b0, w1, b1, emb_tf, offs, out):
     with (
         tc.tile_pool(name="held", bufs=1) as held,
         tc.tile_pool(name="proj", bufs=2) as proj,
-        tc.tile_pool(name="ring", bufs=4) as ring,
+        tc.tile_pool(name="ring", bufs=18) as ring,
         tc.psum_pool(name="psum", bufs=2) as psum,
     ):
         feat_sb = held.tile([P, BLOCKS, ALL_NODES], BF16, name="feat_sb")

@@ -31,8 +31,6 @@ def tile_spmodel_kernel(tc, feat, w0, b0, w1, b1, emb_tf, offs, out):
         nc.sync.dma_start(feat_sb[:], feat.rearrange("(p k) n -> p k n", p=P))
 
         b_sb = [[held.tile([P, 1], F32, name=f"b{i}_sb{cb}") for cb in range(BLOCKS)] for i in range(2)]
-        for i, b in enumerate((b0, b1)):
-            nc.scalar.dma_start(b_sb[i][0][:], b[0:P, :])
 
         offsets = held.tile([P, LIST // STRIPE], U16, name="offsets")
 
@@ -40,9 +38,12 @@ def tile_spmodel_kernel(tc, feat, w0, b0, w1, b1, emb_tf, offs, out):
         emb = [held.tile([P, CODES], F32, name=f"emb{cb}") for cb in range(BLOCKS)]
         for cb in range(BLOCKS):
             channels = slice(cb * P, (cb + 1) * P)
-            nc.sync.dma_start(w_sb[0][cb][:], w0[:, channels].rearrange("(p k) c -> p k c", p=P))
+            first_queue = nc.scalar if cb == 0 else nc.sync
+            first_queue.dma_start(w_sb[0][cb][:], w0[:, channels].rearrange("(p k) c -> p k c", p=P))
             nc.sync.dma_start(w_sb[1][cb][:], w1[:, channels].rearrange("(p k) c -> p k c", p=P))
             if cb == 0:
+                for i, b in enumerate((b0, b1)):
+                    nc.scalar.dma_start(b_sb[i][0][:], b[0:P, :])
                 nc.sync.dma_start(offsets[:], offs)
             nc.sync.dma_start(emb[cb][:], emb_tf[channels, :])
         for cb in range(1, BLOCKS):

@@ -60,11 +60,16 @@ def tile_spmodel_kernel(tc, feat, w0, b0, w1, b1, emb_tf, offs, out):
         def project(cb):
             x = []
             for i in range(2):
+                if cb == 0:
+                    acc_early = psum.tile([P, NODES], F32, name=f"acc{i}_early")
+                    for k in range(BLOCKS):
+                        nc.tensor.matmul(
+                            acc_early[:], w_sb[i][cb][:, k, :], feat_sb[:, k, 0:NODES], start=(k == 0), stop=(k == BLOCKS - 1)
+                        )
+                    nc.vector.tensor_scalar(x_early[i][:], acc_early[:], b_sb[i][0][:], None, ADD)
                 acc = psum.tile([P, ALL_NODES], F32, name=f"acc{i}")
                 for k in range(BLOCKS):
                     nc.tensor.matmul(acc[:], w_sb[i][cb][:, k, :], feat_sb[:, k, :], start=(k == 0), stop=(k == BLOCKS - 1))
-                if cb == 0:
-                    nc.vector.tensor_scalar(x_early[i][:], acc[:, 0:NODES], b_sb[i][0][:], None, ADD)
                 x_sb = proj.tile([P, ALL_NODES], F32, name=f"x{i}_sb")
                 nc.scalar.activation(x_sb[:], acc[:], IDENTITY, bias=b_sb[i][cb][:])
                 x.append(x_sb)
@@ -98,7 +103,7 @@ def tile_spmodel_kernel(tc, feat, w0, b0, w1, b1, emb_tf, offs, out):
             for r in range(GRAPHS):
                 if cb == 0 and r == 0:
                     piece(cb, x_early, r, 0, NODES // 2, pair_on_vector=True)
-                    piece(cb, x, r, NODES // 2, NODES // 2)
+                    piece(cb, x_early, r, NODES // 2, NODES // 2)
                 elif cb == BLOCKS - 1 and r == GRAPHS - 1:
                     piece(cb, x, r, 0, NODES - LAST)
                     piece(cb, x, r, NODES - LAST, LAST)

@@ -17,6 +17,8 @@ STRIPE = 16
 
 FLOPS = 2 * 2 * CHANNELS * CHANNELS * ALL_NODES
 LAST = NODES // 4
+X1_FIRST = 2
+SHARE = NODES // 4
 
 
 def tile_spmodel_kernel(tc, feat, w0, b0, w1, b1, emb_tf, offs, out):
@@ -24,88 +26,125 @@ def tile_spmodel_kernel(tc, feat, w0, b0, w1, b1, emb_tf, offs, out):
     with (
         tc.tile_pool(name="held", bufs=1) as held,
         tc.tile_pool(name="proj", bufs=2) as proj,
-        tc.tile_pool(name="ring", bufs=18) as ring,
+        tc.tile_pool(name="ring", bufs=17) as ring,
+        tc.tile_pool(name="late", bufs=X1_FIRST) as late,
         tc.psum_pool(name="psum", bufs=2) as psum,
+        tc.psum_pool(name="psum_early", bufs=1) as psum_early,
     ):
-        feat_sb = held.tile([P, BLOCKS, ALL_NODES], BF16, name="feat_sb")
-        nc.sync.dma_start(feat_sb[:], feat.rearrange("(p k) n -> p k n", p=P))
-
         b_sb = [[held.tile([P, 1], F32, name=f"b{i}_sb{cb}") for cb in range(BLOCKS)] for i in range(2)]
-
-        offsets = held.tile([P, LIST // STRIPE], U16, name="offsets")
-
         w_sb = [[held.tile([P, BLOCKS, P], BF16, name=f"w{i}_sb{cb}") for cb in range(BLOCKS)] for i in range(2)]
         emb = [held.tile([P, CODES], F32, name=f"emb{cb}") for cb in range(BLOCKS)]
-        for cb in range(BLOCKS):
-            channels = slice(cb * P, (cb + 1) * P)
-            first_queue = nc.scalar if cb == 0 else nc.sync
-            first_queue.dma_start(w_sb[0][cb][:], w0[:, channels].rearrange("(p k) c -> p k c", p=P))
-            nc.sync.dma_start(w_sb[1][cb][:], w1[:, channels].rearrange("(p k) c -> p k c", p=P))
-            if cb == 0:
-                for i, b in enumerate((b0, b1)):
-                    nc.scalar.dma_start(b_sb[i][0][:], b[0:P, :])
-                nc.sync.dma_start(offsets[:], offs)
-            nc.sync.dma_start(emb[cb][:], emb_tf[channels, :])
+        feat_sb = held.tile([P, BLOCKS, ALL_NODES], BF16, name="feat_sb")
+        offsets = held.tile([P, LIST // STRIPE], U16, name="offsets")
+
+        def load_w(queue, i, cb):
+            w = (w0, w1)[i]
+            queue.dma_start(w_sb[i][cb][:], w[:, cb * P : (cb + 1) * P].rearrange("(p k) c -> p k c", p=P))
+
+        def load_b(queue, i, cb):
+            b = (b0, b1)[i]
+            queue.dma_start(b_sb[i][cb][:], b[cb * P : (cb + 1) * P, :])
+
+        load_w(nc.scalar, 1, 0)
+        load_b(nc.scalar, 1, 0)
+        nc.sync.dma_start(feat_sb[:], feat.rearrange("(p k) n -> p k n", p=P))
+        nc.sync.dma_start(offsets[:], offs)
+        nc.sync.dma_start(emb[0][:], emb_tf[0:P, :])
+        load_w(nc.sync, 0, 0)
+        load_b(nc.sync, 0, 0)
         for cb in range(1, BLOCKS):
-            for i, b in enumerate((b0, b1)):
-                nc.sync.dma_start(b_sb[i][cb][:], b[cb * P : (cb + 1) * P, :])
+            load_w(nc.sync, 0, cb)
+            load_w(nc.sync, 1, cb)
+            nc.sync.dma_start(emb[cb][:], emb_tf[cb * P : (cb + 1) * P, :])
+        for cb in range(1, BLOCKS):
+            for i in range(2):
+                load_b(nc.sync, i, cb)
 
         zero = held.tile([P, 1], F32, name="zero")
         warm = held.tile([P, 1], F32, name="warm")
         nc.vector.memset(zero[:], 0.0)
         nc.scalar.activation(warm[:], zero[:], IDENTITY)
 
-        x_early = [held.tile([P, NODES], F32, name=f"x{i}_early") for i in range(2)]
-
-        def project(cb):
-            x = []
-            for i in range(2):
-                if cb == 0:
-                    acc_early = psum.tile([P, NODES], F32, name=f"acc{i}_early")
-                    for k in range(BLOCKS):
-                        nc.tensor.matmul(
-                            acc_early[:], w_sb[i][cb][:, k, :], feat_sb[:, k, 0:NODES], start=(k == 0), stop=(k == BLOCKS - 1)
-                        )
-                    nc.vector.tensor_scalar(x_early[i][:], acc_early[:], b_sb[i][0][:], None, ADD)
-                acc = psum.tile([P, ALL_NODES], F32, name=f"acc{i}")
-                for k in range(BLOCKS):
-                    nc.tensor.matmul(acc[:], w_sb[i][cb][:, k, :], feat_sb[:, k, :], start=(k == 0), stop=(k == BLOCKS - 1))
-                x_sb = proj.tile([P, ALL_NODES], F32, name=f"x{i}_sb")
-                nc.scalar.activation(x_sb[:], acc[:], IDENTITY, bias=b_sb[i][cb][:])
-                x.append(x_sb)
-            return x
-
-        def piece(cb, x, r, a0, many, pair_on_vector=False):
-            nodes = slice(r * NODES, (r + 1) * NODES)
-            width = many * NODES
-            start = r * PAIRS + a0 * NODES
-            pair = ring.tile([P, width], F32, name="pair")
-            if pair_on_vector:
-                nc.vector.tensor_tensor(
-                    pair[:].rearrange("p (a t) -> p a t", a=many),
-                    x[0][:, r * NODES + a0 : r * NODES + a0 + many].unsqueeze(2).to_broadcast([P, many, NODES]),
-                    x[1][:, nodes].unsqueeze(1).to_broadcast([P, many, NODES]),
-                    MULT,
+        def project(acc, i, cb, nodes):
+            for k in range(BLOCKS):
+                nc.tensor.matmul(
+                    acc[:], w_sb[i][cb][:, k, :], feat_sb[:, k, nodes], start=(k == 0), stop=(k == BLOCKS - 1)
                 )
-            else:
-                for a in range(many):
-                    first = r * NODES + a0 + a
-                    nc.scalar.activation(
-                        pair[:, a * NODES : (a + 1) * NODES], x[1][:, nodes], IDENTITY, scale=x[0][:, first : first + 1]
-                    )
-            entries = offsets[:, start // STRIPE : (start + width) // STRIPE]
+
+        def add_bias(acc, i, cb):
+            x_sb = proj.tile([P, ALL_NODES], F32, name=f"x{i}_sb")
+            nc.scalar.activation(x_sb[:], acc[:], IDENTITY, bias=b_sb[i][cb][:])
+            return x_sb
+
+        def times_x0(rows_out, rows_in, x0, r, first_nodes):
+            for a in first_nodes:
+                n = r * NODES + a
+                nc.scalar.activation(rows_out(a), rows_in(a), IDENTITY, scale=x0[:, n : n + 1])
+
+        def look_up(cb, r, a0, many, other):
+            start = r * PAIRS + a0 * NODES
+            width = many * NODES
             prod = ring.tile([P, width], F32, name="prod")
-            nc.vector.tensor_tensor(prod[:], emb[cb][:].indirect(entries), pair[:], MULT)
-            nc.sync.dma_start(out[cb * P : (cb + 1) * P, start : start + width], prod[:])
+            entries = offsets[:, start // STRIPE : (start + width) // STRIPE]
+            nc.vector.tensor_tensor(prod[:], emb[cb][:].indirect(entries), other[:], MULT)
+            return prod
+
+        def store(cb, r, a0, many, tile):
+            start = r * PAIRS + a0 * NODES
+            nc.sync.dma_start(out[cb * P : (cb + 1) * P, start : start + many * NODES], tile[:])
+
+        half = NODES // 2
+        rows = late.tile([P, NODES, NODES], F32, name="rows")
+        early = [psum_early.tile([P, NODES], F32, name=f"early{h}") for h in range(2)]
+        for h in range(2):
+            project(early[h], 1, 0, slice(0, NODES))
+        repeated = [early[h][:].unsqueeze(1).to_broadcast([P, half, NODES]) for h in range(2)]
+        nc.vector.tensor_scalar(rows[:, :half, :], repeated[0], b_sb[1][0][:], None, ADD)
+        nc.scalar.activation(rows[:, half:, :], repeated[1], IDENTITY, bias=b_sb[1][0][:])
+        unfinished = [(0, look_up(0, 0, 0, NODES, rows[:].rearrange("p a t -> p (a t)")))]
+
+        acc1 = psum.tile([P, ALL_NODES], F32, name="acc1")
+        project(acc1, 1, 0, slice(0, ALL_NODES))
+        for r in range(1, X1_FIRST):
+            rows = late.tile([P, NODES, NODES], F32, name="rows")
+            repeated_r = acc1[:, r * NODES : (r + 1) * NODES].unsqueeze(1).to_broadcast([P, NODES, NODES])
+            nc.scalar.activation(rows[:], repeated_r, IDENTITY, bias=b_sb[1][0][:])
+            unfinished.append((r, look_up(0, r, 0, NODES, rows[:].rearrange("p a t -> p (a t)"))))
+        x1 = add_bias(acc1, 1, 0)
+        acc0 = psum.tile([P, ALL_NODES], F32, name="acc0")
+        project(acc0, 0, 0, slice(0, ALL_NODES))
+        x0 = held.tile([P, ALL_NODES], F32, name="x0_first")
+        nc.scalar.activation(x0[:], acc0[:], IDENTITY, bias=b_sb[0][0][:])
+        x0_first = x0
+
+        finished = [late.tile([P, PAIRS], F32, name="finished") for r in range(X1_FIRST)]
+        shares = [(r, prod, a) for r, prod in unfinished for a in range(0, NODES, SHARE)]
+
+        def finish(r, prod, a0):
+            times_x0(
+                lambda a: finished[r][:, a * NODES : (a + 1) * NODES],
+                lambda a: prod[:, a * NODES : (a + 1) * NODES],
+                x0_first, r, range(a0, a0 + SHARE),
+            )
+            if a0 + SHARE == NODES:
+                store(0, r, 0, NODES, finished[r])
 
         for cb in range(BLOCKS):
-            x = project(cb)
-            for r in range(GRAPHS):
-                if cb == 0 and r == 0:
-                    piece(cb, x_early, r, 0, NODES // 2, pair_on_vector=True)
-                    piece(cb, x_early, r, NODES // 2, NODES // 2)
-                elif cb == BLOCKS - 1 and r == GRAPHS - 1:
-                    piece(cb, x, r, 0, NODES - LAST)
-                    piece(cb, x, r, NODES - LAST, LAST)
-                else:
-                    piece(cb, x, r, 0, NODES)
+            if cb > 0:
+                accs = [psum.tile([P, ALL_NODES], F32, name=f"acc{i}") for i in range(2)]
+                for i in range(2):
+                    project(accs[i], i, cb, slice(0, ALL_NODES))
+                x0, x1 = add_bias(accs[0], 0, cb), add_bias(accs[1], 1, cb)
+            for r in range(X1_FIRST if cb == 0 else 0, GRAPHS):
+                last = cb == BLOCKS - 1 and r == GRAPHS - 1
+                for a0, many in ((0, NODES - LAST), (NODES - LAST, LAST)) if last else ((0, NODES),):
+                    pair = ring.tile([P, many * NODES], F32, name="pair")
+                    times_x0(
+                        lambda a: pair[:, (a - a0) * NODES : (a - a0 + 1) * NODES],
+                        lambda a: x1[:, r * NODES : (r + 1) * NODES],
+                        x0, r, range(a0, a0 + many),
+                    )
+                    store(cb, r, a0, many, look_up(cb, r, a0, many, pair))
+                done = cb * GRAPHS + r - X1_FIRST
+                if done < len(shares):
+                    finish(*shares[done])

@@ -25,56 +25,62 @@ def tile_spmodel_kernel(tc, feat, w0, b0, w1, b1, emb_tf, offs, out):
     nc = tc.nc
     with (
         tc.tile_pool(name="held", bufs=1) as held,
-        tc.tile_pool(name="proj", bufs=2) as proj,
+        tc.tile_pool(name="proj", bufs=BLOCKS) as proj,
         tc.tile_pool(name="ring", bufs=17) as ring,
         tc.tile_pool(name="late", bufs=X1_FIRST) as late,
         tc.psum_pool(name="psum", bufs=2) as psum,
         tc.psum_pool(name="psum_early", bufs=1) as psum_early,
     ):
-        b_sb = [[held.tile([P, 1], F32, name=f"b{i}_sb{cb}") for cb in range(BLOCKS)] for i in range(2)]
-        w_sb = [[held.tile([P, BLOCKS, P], BF16, name=f"w{i}_sb{cb}") for cb in range(BLOCKS)] for i in range(2)]
+        rest = BLOCKS - 1
+        b_first = [held.tile([P, 1], F32, name=f"b{i}_first") for i in range(2)]
+        b_rest = [held.tile([P, rest], F32, name=f"b{i}_rest") for i in range(2)]
+        w_first = [held.tile([P, BLOCKS, P], BF16, name=f"w{i}_first") for i in range(2)]
+        w_rest = [held.tile([P, BLOCKS, rest * P], BF16, name=f"w{i}_rest") for i in range(2)]
         emb = [held.tile([P, CODES], F32, name=f"emb{cb}") for cb in range(BLOCKS)]
         feat_sb = held.tile([P, BLOCKS, ALL_NODES], BF16, name="feat_sb")
         offsets = held.tile([P, LIST // STRIPE], U16, name="offsets")
 
-        def load_w(queue, i, cb):
-            w = (w0, w1)[i]
-            queue.dma_start(w_sb[i][cb][:], w[:, cb * P : (cb + 1) * P].rearrange("(p k) c -> p k c", p=P))
+        def load_block_0(queue, i):
+            w, b = ((w0, b0), (w1, b1))[i]
+            queue.dma_start(w_first[i][:], w[:, 0:P].rearrange("(p k) c -> p k c", p=P))
+            queue.dma_start(b_first[i][:], b[0:P, :])
 
-        def load_b(queue, i, cb):
-            b = (b0, b1)[i]
-            queue.dma_start(b_sb[i][cb][:], b[cb * P : (cb + 1) * P, :])
-
-        load_w(nc.scalar, 1, 0)
-        load_b(nc.scalar, 1, 0)
+        load_block_0(nc.scalar, 1)
         nc.sync.dma_start(feat_sb[:], feat.rearrange("(p k) n -> p k n", p=P))
         nc.sync.dma_start(offsets[:], offs)
         nc.sync.dma_start(emb[0][:], emb_tf[0:P, :])
-        load_w(nc.sync, 0, 0)
-        load_b(nc.sync, 0, 0)
+        load_block_0(nc.sync, 0)
+        for i, (w, b) in enumerate(((w0, b0), (w1, b1))):
+            nc.sync.dma_start(w_rest[i][:], w[:, P:CHANNELS].rearrange("(p k) c -> p k c", p=P))
+            nc.sync.dma_start(b_rest[i][:], b[P:CHANNELS, :].rearrange("(a p) o -> p (a o)", p=P))
         for cb in range(1, BLOCKS):
-            load_w(nc.sync, 0, cb)
-            load_w(nc.sync, 1, cb)
             nc.sync.dma_start(emb[cb][:], emb_tf[cb * P : (cb + 1) * P, :])
-        for cb in range(1, BLOCKS):
-            for i in range(2):
-                load_b(nc.sync, i, cb)
 
         zero = held.tile([P, 1], F32, name="zero")
         warm = held.tile([P, 1], F32, name="warm")
         nc.vector.memset(zero[:], 0.0)
         nc.scalar.activation(warm[:], zero[:], IDENTITY)
 
+        def weights(i, cb, k):
+            return w_first[i][:, k, :] if cb == 0 else w_rest[i][:, k, (cb - 1) * P : cb * P]
+
+        def bias(i, cb):
+            return b_first[i][:] if cb == 0 else b_rest[i][:, cb - 1 : cb]
+
         def project(acc, i, cb, nodes):
             for k in range(BLOCKS):
-                nc.tensor.matmul(
-                    acc[:], w_sb[i][cb][:, k, :], feat_sb[:, k, nodes], start=(k == 0), stop=(k == BLOCKS - 1)
-                )
+                nc.tensor.matmul(acc[:], weights(i, cb, k), feat_sb[:, k, nodes], start=(k == 0), stop=(k == BLOCKS - 1))
 
         def add_bias(acc, i, cb):
             x_sb = proj.tile([P, ALL_NODES], F32, name=f"x{i}_sb")
-            nc.scalar.activation(x_sb[:], acc[:], IDENTITY, bias=b_sb[i][cb][:])
+            nc.scalar.activation(x_sb[:], acc[:], IDENTITY, bias=bias(i, cb))
             return x_sb
+
+        def linear_maps(cb):
+            accs = [psum.tile([P, ALL_NODES], F32, name=f"acc{i}") for i in range(2)]
+            for i in range(2):
+                project(accs[i], i, cb, slice(0, ALL_NODES))
+            return [add_bias(accs[i], i, cb) for i in range(2)]
 
         def times_x0(rows_out, rows_in, x0, r, first_nodes):
             for a in first_nodes:
@@ -99,8 +105,8 @@ def tile_spmodel_kernel(tc, feat, w0, b0, w1, b1, emb_tf, offs, out):
         for h in range(2):
             project(early[h], 1, 0, slice(0, NODES))
         repeated = [early[h][:].unsqueeze(1).to_broadcast([P, half, NODES]) for h in range(2)]
-        nc.vector.tensor_scalar(rows[:, :half, :], repeated[0], b_sb[1][0][:], None, ADD)
-        nc.scalar.activation(rows[:, half:, :], repeated[1], IDENTITY, bias=b_sb[1][0][:])
+        nc.vector.tensor_scalar(rows[:, :half, :], repeated[0], bias(1, 0), None, ADD)
+        nc.scalar.activation(rows[:, half:, :], repeated[1], IDENTITY, bias=bias(1, 0))
         unfinished = [(0, look_up(0, 0, 0, NODES, rows[:].rearrange("p a t -> p (a t)")))]
 
         acc1 = psum.tile([P, ALL_NODES], F32, name="acc1")
@@ -108,14 +114,12 @@ def tile_spmodel_kernel(tc, feat, w0, b0, w1, b1, emb_tf, offs, out):
         for r in range(1, X1_FIRST):
             rows = late.tile([P, NODES, NODES], F32, name="rows")
             repeated_r = acc1[:, r * NODES : (r + 1) * NODES].unsqueeze(1).to_broadcast([P, NODES, NODES])
-            nc.scalar.activation(rows[:], repeated_r, IDENTITY, bias=b_sb[1][0][:])
+            nc.scalar.activation(rows[:], repeated_r, IDENTITY, bias=bias(1, 0))
             unfinished.append((r, look_up(0, r, 0, NODES, rows[:].rearrange("p a t -> p (a t)"))))
         x1 = add_bias(acc1, 1, 0)
         acc0 = psum.tile([P, ALL_NODES], F32, name="acc0")
         project(acc0, 0, 0, slice(0, ALL_NODES))
-        x0 = held.tile([P, ALL_NODES], F32, name="x0_first")
-        nc.scalar.activation(x0[:], acc0[:], IDENTITY, bias=b_sb[0][0][:])
-        x0_first = x0
+        x = [(add_bias(acc0, 0, 0), x1)]
 
         finished = [late.tile([P, PAIRS], F32, name="finished") for r in range(X1_FIRST)]
         shares = [(r, prod, a) for r, prod in unfinished for a in range(0, NODES, SHARE)]
@@ -124,19 +128,17 @@ def tile_spmodel_kernel(tc, feat, w0, b0, w1, b1, emb_tf, offs, out):
             times_x0(
                 lambda a: finished[r][:, a * NODES : (a + 1) * NODES],
                 lambda a: prod[:, a * NODES : (a + 1) * NODES],
-                x0_first, r, range(a0, a0 + SHARE),
+                x[0][0], r, range(a0, a0 + SHARE),
             )
             if a0 + SHARE == NODES:
                 store(0, r, 0, NODES, finished[r])
 
         for cb in range(BLOCKS):
-            if cb > 0:
-                accs = [psum.tile([P, ALL_NODES], F32, name=f"acc{i}") for i in range(2)]
-                for i in range(2):
-                    project(accs[i], i, cb, slice(0, ALL_NODES))
-                x0, x1 = add_bias(accs[0], 0, cb), add_bias(accs[1], 1, cb)
+            x0, x1 = x[cb]
             for r in range(X1_FIRST if cb == 0 else 0, GRAPHS):
                 last = cb == BLOCKS - 1 and r == GRAPHS - 1
+                if r == GRAPHS - 1 and not last:
+                    x.append(linear_maps(cb + 1))
                 for a0, many in ((0, NODES - LAST), (NODES - LAST, LAST)) if last else ((0, NODES),):
                     pair = ring.tile([P, many * NODES], F32, name="pair")
                     times_x0(

@@ -16,7 +16,7 @@ BLOCKS = CHANNELS // P
 STRIPE = 16
 
 FLOPS = 2 * 2 * CHANNELS * CHANNELS * ALL_NODES
-LAST = NODES // 4
+LAST = NODES * 3 // 8
 X1_FIRST = 2
 SHARE = NODES // 4
 
@@ -40,16 +40,21 @@ def tile_spmodel_kernel(tc, feat, w0, b0, w1, b1, emb_tf, offs, out):
         feat_sb = held.tile([P, BLOCKS, ALL_NODES], BF16, name="feat_sb")
         offsets = held.tile([P, LIST // STRIPE], U16, name="offsets")
 
-        def load_block_0(queue, i):
-            w, b = ((w0, b0), (w1, b1))[i]
-            queue.dma_start(w_first[i][:], w[:, 0:P].rearrange("(p k) c -> p k c", p=P))
-            queue.dma_start(b_first[i][:], b[0:P, :])
+        def load_w_first(queue, i, ks):
+            columns = (w0, w1)[i][:, 0:P].rearrange("(p k) c -> p k c", p=P)
+            queue.dma_start(w_first[i][:, ks, :], columns[:, ks, :])
 
-        load_block_0(nc.scalar, 1)
+        def load_b_first(queue, i):
+            queue.dma_start(b_first[i][:], (b0, b1)[i][0:P, :])
+
+        load_w_first(nc.scalar, 1, slice(0, BLOCKS // 2))
+        load_b_first(nc.scalar, 1)
         nc.sync.dma_start(feat_sb[:], feat.rearrange("(p k) n -> p k n", p=P))
+        load_w_first(nc.sync, 1, slice(BLOCKS // 2, BLOCKS))
         nc.sync.dma_start(offsets[:], offs)
         nc.sync.dma_start(emb[0][:], emb_tf[0:P, :])
-        load_block_0(nc.sync, 0)
+        load_w_first(nc.sync, 0, slice(0, BLOCKS))
+        load_b_first(nc.sync, 0)
         for i, (w, b) in enumerate(((w0, b0), (w1, b1))):
             nc.sync.dma_start(w_rest[i][:], w[:, P:CHANNELS].rearrange("(p k) c -> p k c", p=P))
             nc.sync.dma_start(b_rest[i][:], b[P:CHANNELS, :].rearrange("(a p) o -> p (a o)", p=P))

@@ -72,9 +72,12 @@ def tile_spmodel_kernel(tc, feat, w0, b0, w1, b1, emb_tf, offs, out):
         def bias(i, cb):
             return b_first[i][:] if cb == 0 else b_rest[i][:, cb - 1 : cb]
 
-        def project(acc, i, cb, nodes):
+        def project(accs, i, cb, nodes):
             for k in range(BLOCKS):
-                nc.tensor.matmul(acc[:], weights(i, cb, k), feat_sb[:, k, nodes], start=(k == 0), stop=(k == BLOCKS - 1))
+                for acc in accs:
+                    nc.tensor.matmul(
+                        acc[:], weights(i, cb, k), feat_sb[:, k, nodes], start=(k == 0), stop=(k == BLOCKS - 1)
+                    )
 
         def add_bias(acc, i, cb):
             x_sb = proj.tile([P, ALL_NODES], F32, name=f"x{i}_sb")
@@ -84,7 +87,7 @@ def tile_spmodel_kernel(tc, feat, w0, b0, w1, b1, emb_tf, offs, out):
         def linear_maps(cb):
             accs = [psum.tile([P, ALL_NODES], F32, name=f"acc{i}") for i in range(2)]
             for i in range(2):
-                project(accs[i], i, cb, slice(0, ALL_NODES))
+                project([accs[i]], i, cb, slice(0, ALL_NODES))
             return [add_bias(accs[i], i, cb) for i in range(2)]
 
         def times_x0(rows_out, rows_in, x0, r, first_nodes):
@@ -107,15 +110,14 @@ def tile_spmodel_kernel(tc, feat, w0, b0, w1, b1, emb_tf, offs, out):
         half = NODES // 2
         rows = late.tile([P, NODES, NODES], F32, name="rows")
         early = [psum_early.tile([P, NODES], F32, name=f"early{h}") for h in range(2)]
-        for h in range(2):
-            project(early[h], 1, 0, slice(0, NODES))
+        project(early, 1, 0, slice(0, NODES))
         repeated = [early[h][:].unsqueeze(1).to_broadcast([P, half, NODES]) for h in range(2)]
         nc.vector.tensor_scalar(rows[:, :half, :], repeated[0], bias(1, 0), None, ADD)
         nc.scalar.activation(rows[:, half:, :], repeated[1], IDENTITY, bias=bias(1, 0))
         unfinished = [(0, look_up(0, 0, 0, NODES, rows[:].rearrange("p a t -> p (a t)")))]
 
         acc1 = psum.tile([P, ALL_NODES], F32, name="acc1")
-        project(acc1, 1, 0, slice(0, ALL_NODES))
+        project([acc1], 1, 0, slice(0, ALL_NODES))
         for r in range(1, X1_FIRST):
             rows = late.tile([P, NODES, NODES], F32, name="rows")
             repeated_r = acc1[:, r * NODES : (r + 1) * NODES].unsqueeze(1).to_broadcast([P, NODES, NODES])
@@ -123,7 +125,7 @@ def tile_spmodel_kernel(tc, feat, w0, b0, w1, b1, emb_tf, offs, out):
             unfinished.append((r, look_up(0, r, 0, NODES, rows[:].rearrange("p a t -> p (a t)"))))
         x1 = add_bias(acc1, 1, 0)
         acc0 = psum.tile([P, ALL_NODES], F32, name="acc0")
-        project(acc0, 0, 0, slice(0, ALL_NODES))
+        project([acc0], 0, 0, slice(0, ALL_NODES))
         x = [(add_bias(acc0, 0, 0), x1)]
 
         finished = [late.tile([P, PAIRS], F32, name="finished") for r in range(X1_FIRST)]

import concourse.mybir as mybir

BF16, F32, U16 = mybir.dt.bfloat16, mybir.dt.float32, mybir.dt.uint16
MULT, ADD = mybir.AluOpType.mult, mybir.AluOpType.add
IDENTITY = mybir.ActivationFunctionType.Identity

P = 128
CHANNELS = 512
CODES = 1024
GRAPHS = 4
NODES = 32
ALL_NODES = GRAPHS * NODES
PAIRS = NODES * NODES
LIST = GRAPHS * PAIRS
BLOCKS = CHANNELS // P
STRIPE = 16

FLOPS = 2 * 2 * CHANNELS * CHANNELS * ALL_NODES
LAST = NODES * 3 // 8
X1_FIRST = 2
SHARE = NODES // 4


def tile_spmodel_kernel(tc, feat, w0, b0, w1, b1, emb_tf, offs, out):
    nc = tc.nc
    with (
        tc.tile_pool(name="held", bufs=1) as held,
        tc.tile_pool(name="proj", bufs=BLOCKS) as proj,
        tc.tile_pool(name="ring", bufs=17) as ring,
        tc.tile_pool(name="late", bufs=X1_FIRST) as late,
        tc.psum_pool(name="psum", bufs=2) as psum,
        tc.psum_pool(name="psum_early", bufs=1) as psum_early,
    ):
        rest = BLOCKS - 1
        b_first = [held.tile([P, 1], F32, name=f"b{i}_first") for i in range(2)]
        b_rest = [held.tile([P, rest], F32, name=f"b{i}_rest") for i in range(2)]
        w_first = [held.tile([P, BLOCKS, P], BF16, name=f"w{i}_first") for i in range(2)]
        w_rest = [held.tile([P, BLOCKS, rest * P], BF16, name=f"w{i}_rest") for i in range(2)]
        emb = [held.tile([P, CODES], F32, name=f"emb{cb}") for cb in range(BLOCKS)]
        feat_sb = held.tile([P, BLOCKS, ALL_NODES], BF16, name="feat_sb")
        offsets = held.tile([P, LIST // STRIPE], U16, name="offsets")

        def load_w_first(queue, i, ks):
            columns = (w0, w1)[i][:, 0:P].rearrange("(p k) c -> p k c", p=P)
            queue.dma_start(w_first[i][:, ks, :], columns[:, ks, :])

        def load_b_first(queue, i):
            queue.dma_start(b_first[i][:], (b0, b1)[i][0:P, :])

        load_w_first(nc.scalar, 1, slice(0, BLOCKS // 2))
        load_b_first(nc.scalar, 1)
        nc.sync.dma_start(feat_sb[:], feat.rearrange("(p k) n -> p k n", p=P))
        load_w_first(nc.sync, 1, slice(BLOCKS // 2, BLOCKS))
        nc.sync.dma_start(offsets[:], offs)
        nc.sync.dma_start(emb[0][:], emb_tf[0:P, :])
        load_w_first(nc.sync, 0, slice(0, BLOCKS))
        load_b_first(nc.sync, 0)
        for i, (w, b) in enumerate(((w0, b0), (w1, b1))):
            nc.sync.dma_start(w_rest[i][:], w[:, P:CHANNELS].rearrange("(p k) c -> p k c", p=P))
            nc.sync.dma_start(b_rest[i][:], b[P:CHANNELS, :].rearrange("(a p) o -> p (a o)", p=P))
        for cb in range(1, BLOCKS):
            nc.sync.dma_start(emb[cb][:], emb_tf[cb * P : (cb + 1) * P, :])

        zero = held.tile([P, 1], F32, name="zero")
        warm = held.tile([P, 1], F32, name="warm")
        nc.vector.memset(zero[:], 0.0)
        nc.scalar.activation(warm[:], zero[:], IDENTITY)

        def weights(i, cb, k):
            return w_first[i][:, k, :] if cb == 0 else w_rest[i][:, k, (cb - 1) * P : cb * P]

        def bias(i, cb):
            return b_first[i][:] if cb == 0 else b_rest[i][:, cb - 1 : cb]

        def project(accs, i, cb, nodes):
            for k in range(BLOCKS):
                for acc in accs:
                    nc.tensor.matmul(
                        acc[:], weights(i, cb, k), feat_sb[:, k, nodes], start=(k == 0), stop=(k == BLOCKS - 1)
                    )

        def add_bias(acc, i, cb):
            x_sb = proj.tile([P, ALL_NODES], F32, name=f"x{i}_sb")
            nc.scalar.activation(x_sb[:], acc[:], IDENTITY, bias=bias(i, cb))
            return x_sb

        def linear_maps(cb):
            accs = [psum.tile([P, ALL_NODES], F32, name=f"acc{i}") for i in range(2)]
            for i in range(2):
                project([accs[i]], i, cb, slice(0, ALL_NODES))
            return [add_bias(accs[i], i, cb) for i in range(2)]

        def times_x0(rows_out, rows_in, x0, r, first_nodes):
            for a in first_nodes:
                n = r * NODES + a
                nc.scalar.activation(rows_out(a), rows_in(a), IDENTITY, scale=x0[:, n : n + 1])

        def look_up(cb, r, a0, many, other):
            start = r * PAIRS + a0 * NODES
            width = many * NODES
            prod = ring.tile([P, width], F32, name="prod")
            entries = offsets[:, start // STRIPE : (start + width) // STRIPE]
            nc.vector.tensor_tensor(prod[:], emb[cb][:].indirect(entries), other[:], MULT)
            return prod

        def store(cb, r, a0, many, tile):
            start = r * PAIRS + a0 * NODES
            nc.sync.dma_start(out[cb * P : (cb + 1) * P, start : start + many * NODES], tile[:])

        half = NODES // 2
        rows = late.tile([P, NODES, NODES], F32, name="rows")
        early = [psum_early.tile([P, NODES], F32, name=f"early{h}") for h in range(2)]
        project(early, 1, 0, slice(0, NODES))
        repeated = [early[h][:].unsqueeze(1).to_broadcast([P, half, NODES]) for h in range(2)]
        nc.vector.tensor_scalar(rows[:, :half, :], repeated[0], bias(1, 0), None, ADD)
        nc.scalar.activation(rows[:, half:, :], repeated[1], IDENTITY, bias=bias(1, 0))
        unfinished = [(0, look_up(0, 0, 0, NODES, rows[:].rearrange("p a t -> p (a t)")))]

        acc1 = psum.tile([P, ALL_NODES], F32, name="acc1")
        project([acc1], 1, 0, slice(0, ALL_NODES))
        for r in range(1, X1_FIRST):
            rows = late.tile([P, NODES, NODES], F32, name="rows")
            repeated_r = acc1[:, r * NODES : (r + 1) * NODES].unsqueeze(1).to_broadcast([P, NODES, NODES])
            nc.scalar.activation(rows[:], repeated_r, IDENTITY, bias=bias(1, 0))
            unfinished.append((r, look_up(0, r, 0, NODES, rows[:].rearrange("p a t -> p (a t)"))))
        x1 = add_bias(acc1, 1, 0)
        acc0 = psum.tile([P, ALL_NODES], F32, name="acc0")
        project([acc0], 0, 0, slice(0, ALL_NODES))
        x = [(add_bias(acc0, 0, 0), x1)]

        finished = [late.tile([P, PAIRS], F32, name="finished") for r in range(X1_FIRST)]
        shares = [(r, prod, a) for r, prod in unfinished for a in range(0, NODES, SHARE)]

        def finish(r, prod, a0):
            times_x0(
                lambda a: finished[r][:, a * NODES : (a + 1) * NODES],
                lambda a: prod[:, a * NODES : (a + 1) * NODES],
                x[0][0], r, range(a0, a0 + SHARE),
            )
            if a0 + SHARE == NODES:
                store(0, r, 0, NODES, finished[r])

        for cb in range(BLOCKS):
            x0, x1 = x[cb]
            for r in range(X1_FIRST if cb == 0 else 0, GRAPHS):
                last = cb == BLOCKS - 1 and r == GRAPHS - 1
                if r == GRAPHS - 1 and not last:
                    x.append(linear_maps(cb + 1))
                for a0, many in ((0, NODES - LAST), (NODES - LAST, LAST)) if last else ((0, NODES),):
                    pair = ring.tile([P, many * NODES], F32, name="pair")
                    times_x0(
                        lambda a: pair[:, (a - a0) * NODES : (a - a0 + 1) * NODES],
                        lambda a: x1[:, r * NODES : (r + 1) * NODES],
                        x0, r, range(a0, a0 + many),
                    )
                    store(cb, r, a0, many, look_up(cb, r, a0, many, pair))
                done = cb * GRAPHS + r - X1_FIRST
                if done < len(shares):
                    finish(*shares[done])
